import numpy as np
import ml_dtypes


def mxq(x, axis, fmt="e4m3"):
    dtype, down = {"e4m3": (ml_dtypes.float8_e4m3fn, 7), "e5m2": (ml_dtypes.float8_e5m2, 14)}[fmt]
    v = np.moveaxis(np.asarray(x, np.float32).astype(ml_dtypes.bfloat16).astype(np.float64), axis, -1)
    blocks = v.reshape(v.shape[:-1] + (-1, 32))
    amax = np.abs(blocks).max(-1, keepdims=True)
    byte = np.maximum(np.where(amax > 0, np.frexp(amax)[1] - 1 + 127, 0) - down, 1)
    scale = np.exp2(byte - 127.0)
    codes = (blocks / scale).astype(np.float32).astype(dtype).astype(np.float64)
    return np.moveaxis((codes * scale).reshape(v.shape), -1, axis)


WIDE = False


def mx_kscale(k):
    if not WIDE:
        return np.ones(k)
    levels = np.array([10, -10, 5, -5, 0])
    if k % 512:
        return np.exp2(np.random.permutation(np.resize(levels, k // 32))).repeat(32)
    a = np.empty((k // 512, 16))
    for p in range(k // 512):
        a[p, :8] = np.random.permutation(np.resize(levels, 8))
        for g in range(8):
            far = levels[np.abs(levels - a[p, g]) >= 10]
            a[p, g + 8] = far[np.random.randint(len(far))]
    return np.exp2(a.ravel()).repeat(32)


BF16 = ml_dtypes.bfloat16


def bf(x):
    return np.asarray(x, np.float32).astype(BF16)


def f64(x):
    return np.asarray(x).astype(np.float64)


N, IN_DIM, HID, OUT_DIM = 1024, 1024, 512, 256
CAT = 3 * HID


def log_softmax(v):
    d = v - v.max(-1, keepdims=True)
    return d - np.log(np.exp(d).sum(-1, keepdims=True))


def draw0():
    s, t = mx_kscale(HID), mx_kscale(CAT)
    ta, tb, tc = t[:HID], t[HID:2 * HID], t[2 * HID:]
    return {"u1": bf(np.maximum(np.random.standard_normal((N, HID)) * 2.0, 0.0) * s),
            "W2_1": bf(np.random.standard_normal((HID, HID)) * 0.5 / np.sqrt(HID) / s[:, None] * tc),
            "b2_1": bf(np.random.standard_normal(HID) * 0.3 * tc),
            "h": bf(np.random.standard_normal((N, HID)) * ta),
            "h1": bf(np.random.standard_normal((N, HID)) * 0.8 * tb),
            "W_out": bf(np.random.standard_normal((CAT, OUT_DIM)) * 2.0 / np.sqrt(CAT) / t[:, None]),
            "b_out": bf(np.random.standard_normal(OUT_DIM) * 0.3)}


def core(u1, W2_1, b2_1, h, h1, W_out, b_out):
    h2 = (mxq(f64(u1), 1, "e4m3") @ mxq(f64(W2_1), 0, "e4m3")) + f64(b2_1)
    cat = np.concatenate([f64(h), f64(h1), h2], axis=-1)
    logits = (mxq(cat, 1, "e4m3") @ mxq(f64(W_out), 0, "e4m3")) + f64(b_out)
    return log_softmax(logits)


def e4m3fn_bytes(y):
    return np.clip(np.asarray(y, np.float64), -448.0, 448.0).astype(np.float32).astype(ml_dtypes.float8_e4m3fn).view(np.uint8)


def e4m3fn_values(b):
    return np.asarray(b, np.uint8).view(ml_dtypes.float8_e4m3fn).astype(np.float64)


def setup_inputs():
    d = draw0()
    x0 = np.asarray(d['u1']).astype(np.float64)
    s = (np.max(np.abs(x0), axis=(0,), keepdims=True) / 448.0).astype(np.float32)
    out = {}
    for k, v in d.items():
        if k == 'u1':
            out['u1_bytes'] = e4m3fn_bytes(x0 / s.astype(np.float64))
            out['u1_scale'] = s
        else:
            out[k] = v
    return out


def reference(u1_bytes, u1_scale, W2_1, b2_1, h, h1, W_out, b_out):
    return core(e4m3fn_values(u1_bytes) * u1_scale.astype(np.float64), W2_1, b2_1, h, h1, W_out, b_out)

@@ -1,0 +1,253 @@
+from contextlib import ExitStack
+
+import concourse.mybir as mybir
+from concourse.masks import make_identity
+
+F32 = mybir.dt.float32
+BF16 = mybir.dt.bfloat16
+U32 = mybir.dt.uint32
+U8 = mybir.dt.uint8
+FP8 = mybir.dt.float8_e4m3fn
+FP8X4 = mybir.dt.float8_e4m3fn_x4
+ALU = mybir.AluOpType
+ACT = mybir.ActivationFunctionType
+AX = mybir.AxisListType
+
+N, HID, CLS = 1024, 512, 256
+P = 128
+G = N // P
+ORDER = """ldw2.x.0 ldu.x.0 ldu.x.1 lduh.x.1 ldwo.x.0 ldh.x.0 ldg.x.0 ldwx.x.0 ldh.x.1 ldg.x.1
+scP.p.0 boF.v.0 boP.p.0 sc.s.0 w2i.v.0 w2i.s.1 tt.v.1 w2i.s.3 tt.v.0 bo.s.0 tt.v.5 tru.p.0 w2i.s.2 tt.v.4 woi.s.0 tt.v.3 tru.p.2 tt.v.2 trh.p.0 cpu.s.0 qw2.v.0 cpu.s.2 tru.p.1 qup.v.0 qwo.v.0 cph.s.0 trh.p.1 qup.v.2 tt.v.7 cpu.s.1 s1.p.1 s1.p.4 tt.v.6 woi.s.1 s1.p.5 trg.p.1 h2.v.1 h2.v.5 trh.p.2 woi.s.2 qwo.v.1 s1.p.0 qup.v.1 h2.v.4 s1.p.2 cpg.s.1 qwo.v.2 s1.p.3 cph.s.1 qh2.v.2 trg.p.2 h2.v.0 cph.s.2 tru.p.3 qh.v.1 cpg.s.2 trg.p.3 qh2.v.0 cpu.s.3 h2.v.2 trh.p.3 cpg.s.3 trg.p.0 qh.v.2 cph.s.3 qup.v.3 s2.p.2 h2.v.3 cpg.s.0 qh.v.3 s1.p.6 s1.p.7 lt.v.2 qh.v.0 mx.v.2 s2.p.0 h2.v.6 ex.s.4 ex.s.5 qh2.v.1 h2.v.7 s2.p.1 lt.v.0 qh2.v.3 lt.v.1 s2.p.3 mx.v.0 mx.v.1 ex.s.1 ex.s.0 lt1.v.6 ex.s.2 lt1.v.7 mx1.v.6 ex.s.3 mx1.v.7 ex.s.6 ex.s.7 ln.s.0 fin.v.2 fin.v.3 fin.v.0 fin.v.5 fin.v.4 fin.v.1 sh.v.0 fin.s.6 st.y.1 fin.s.7 st.y.2 st.y.0 st.y.3""".split()
+GROUPS = [[0,8]]
+FLOPS = 2 * N * HID * HID + 2 * N * 3 * HID * CLS
+
+
+def tile_gin_pc_kernel(tc, u1_bytes, u1_scale, W2_1, b2_1, h, h1, W_out, b_out, out):
+    nc = tc.nc
+    with ExitStack() as ctx:
+        keep = ctx.enter_context(tc.tile_pool(name="keep", bufs=1))
+        work = ctx.enter_context(tc.tile_pool(name="work", bufs=3))
+        psum = ctx.enter_context(tc.psum_pool(name="psum", bufs=2))
+        ctx.enter_context(tc.manual_schedule())
+
+        def kt(name, shape, dtype):
+            return keep.tile(shape, dtype, name=name, align_bytes=64)
+
+        u1b = kt("u1b", [P, G, HID], U8)
+        w2r = kt("w2r", [P, 4, HID], BF16)
+        wor = kt("wor", [P, 3, 4, CLS], BF16)
+        hr = kt("hr", [P, G, HID], BF16)
+        h1r = kt("h1r", [P, G, HID], BF16)
+        sccol = kt("sccol", [P, 4], F32)
+        b2 = kt("b2", [P, 4], BF16)
+        bocol = kt("bocol", [P, 2], BF16)
+        bocf = kt("bocf", [P, 2], F32)
+        sc = kt("sc", [P, HID], F32)
+        bo = kt("bo", [P, CLS], F32)
+        ident = kt("ident", [P, P], F32)
+        w2g = kt("w2g", [P, HID, 4], BF16)
+        wog = kt("wog", [P, 3, CLS, 4], BF16)
+        w2c = kt("w2c", [P, HID], U32)
+        w2s = kt("w2s", [P, HID], U8)
+        woc = kt("woc", [P, 3, CLS], U32)
+        wos = kt("wos", [P, 3, CLS], U8)
+        uc = kt("uc", [P, N], U32)
+        us = kt("us", [P, N], U8)
+        cc = kt("cc", [P, 2 * N], U32)
+        cs = kt("cs", [P, 2 * N], U8)
+        c2 = kt("c2", [P, N], U32)
+        s2 = kt("s2c", [P, N], U8)
+        L = kt("L", [P, G, CLS], F32)
+        res = kt("res", [P, G, CLS], F32)
+        nmax = kt("nmax", [P, G], F32)
+        sums = kt("sums", [P, G], F32)
+        lns = kt("lns", [P, G], F32)
+        shift = kt("shift", [P, G], F32)
+        dummy = kt("dummy", [P, 1], F32)
+
+        nc.scalar.dma_start(out=sccol[:], in_=u1_scale.rearrange("o (p t) -> p (o t)", t=4))
+        nc.scalar.dma_start(out=bocol[:], in_=b_out.rearrange("(p t) -> p t", t=2))
+        nc.scalar.dma_start(out=b2[:], in_=b2_1.rearrange("(p t) -> p t", t=4))
+        u1v = u1_bytes.rearrange("(p g) k -> p g k", g=G)
+        hv = h.rearrange("(p g) k -> p g k", g=G)
+        h1v = h1.rearrange("(p g) k -> p g k", g=G)
+        ov = out.rearrange("(p g) c -> p g c", g=G)
+        wov = W_out.rearrange("(c p j) n -> p c j n", p=P, j=4)
+        w2v = W2_1.rearrange("(p j) n -> p j n", j=4)
+
+        nc.vector.memset(dummy[:], 0.0)
+        nc.scalar.activation(out=dummy[:], in_=dummy[:], func=ACT.Exp)
+        make_identity(nc, ident[:])
+
+        xs, ug, hg, h2g, s1b, s2b, trb, hp = {}, {}, {}, {}, {}, {}, {}, {}
+        raw = [hr, h1r]
+
+        def cp(eng, out, in_):
+            if eng == "v":
+                nc.vector.tensor_copy(out=out, in_=in_)
+            elif eng == "g":
+                nc.gpsimd.tensor_scalar(out=out, in0=in_, scalar1=1.0, scalar2=0.0, op0=ALU.mult, op1=ALU.add)
+            else:
+                nc.scalar.copy(out=out, in_=in_)
+
+        def quant(codes, scales, src):
+            nc.vector.quantize_mx(out=codes.bitcast(FP8X4), scales=scales, in_=src)
+
+        def turn(views):
+            b = psum.tile([P, len(views), 2, P], F32, name="tr", bufs=3)
+            for i, w in enumerate(views):
+                for u in range(2):
+                    nc.tensor.transpose(b[:, i, u, :], w[:, u : HID // 2 : 2], ident[:])
+            return b
+
+        def drain(eng, b, o):
+            ow = o.rearrange("p n j -> p (n j)").bitcast(F32).rearrange("p (i r u) -> p i r u", i=2, u=2)
+            cp(eng, ow, b[:].rearrange("p i u r -> p i r u"))
+
+        def step(op, eng, i):
+            if op == "ldw2":
+                nc.sync.dma_start(out=w2r[:], in_=w2v)
+            elif op == "ldu":
+                nc.sync.dma_start(out=u1b[:, 2 * i : 2 * i + 2, :], in_=u1v[:, 2 * i : 2 * i + 2, :])
+            elif op == "lduh":
+                nc.sync.dma_start(out=u1b[:, 4 * i : 4 * i + 4, :], in_=u1v[:, 4 * i : 4 * i + 4, :])
+            elif op == "ldh":
+                nc.sync.dma_start(out=hr[:, 4 * i : 4 * i + 4, :], in_=hv[:, 4 * i : 4 * i + 4, :])
+            elif op == "ldg":
+                nc.sync.dma_start(out=h1r[:, 4 * i : 4 * i + 4, :], in_=h1v[:, 4 * i : 4 * i + 4, :])
+            elif op == "ldwo":
+                nc.sync.dma_start(out=wor[:, i], in_=wov[:, i])
+            elif op == "ldwx":
+                nc.sync.dma_start(out=wor[:, 1:3], in_=wov[:, 1:3])
+            elif op == "scP":
+                trb["sc"] = psum.tile([P, 4, P], F32, name="tr", bufs=3)
+                for t in range(4):
+                    nc.tensor.transpose(trb["sc"][:, t, :], sccol[:, t : t + 1].to_broadcast([P, P]), ident[:])
+            elif op == "sc":
+                cp(eng, sc[:].rearrange("p (q t) -> p q t", t=4), trb["sc"][:].rearrange("p t q -> p q t"))
+            elif op == "boF":
+                nc.vector.tensor_copy(out=bocf[:], in_=bocol[:])
+            elif op == "boP":
+                trb["bo"] = psum.tile([P, 4, P], F32, name="tr", bufs=3)
+                for t in range(2):
+                    nc.tensor.transpose(trb["bo"][:, t, :], bocf[:, t : t + 1].to_broadcast([P, P]), ident[:])
+            elif op == "bo":
+                cp(eng, bo[:].rearrange("p (q t) -> p q t", t=2), trb["bo"][:, 0:2, :].rearrange("p t q -> p q t"))
+            elif op == "w2i":
+                cp(eng, w2g[:, i * P : (i + 1) * P, :], w2r[:].rearrange("p j (m t) -> p t m j", t=4)[:, i])
+            elif op == "woi":
+                cp(eng, wog[:, i], wor[:, i].rearrange("p j n -> p n j"))
+            elif op == "qw2":
+                quant(w2c[:], w2s[:], w2g[:].rearrange("p n j -> p (n j)"))
+            elif op == "qwo":
+                quant(woc[:, i, :], wos[:, i, :], wog[:, i].rearrange("p n j -> p (n j)"))
+            elif op == "tt":
+                xs[i] = work.tile([P, HID], BF16, name="xs", bufs=8, align_bytes=64)
+                nc.vector.tensor_tensor(out=xs[i][:], in0=u1b[:, i, :].bitcast(FP8), in1=sc[:], op=ALU.mult)
+            elif op == "tru":
+                trb["u", i] = turn([xs[2 * i + k][:].bitcast(F32) for k in range(2)])
+            elif op == "cpu":
+                if i // 2 not in ug:
+                    ug[i // 2] = work.tile([P, 4 * P, 4], BF16, name="ug", bufs=2, align_bytes=64)
+                drain(eng, trb["u", i], ug[i // 2][:, 2 * P * (i % 2) : 2 * P * (i % 2) + 2 * P, :])
+            elif op == "qu":
+                s = slice(512 * i, 512 * i + 512)
+                quant(uc[:, s], us[:, s], ug[i][:].rearrange("p n j -> p (n j)"))
+            elif op == "qup":
+                s = slice(256 * i, 256 * i + 256)
+                quant(uc[:, s], us[:, s], ug[i // 2][:, 256 * (i % 2) : 256 * (i % 2) + 256, :].rearrange("p n j -> p (n j)"))
+            elif op in ("trh", "trg"):
+                r = raw[op == "trg"]
+                trb[op, i] = turn([r[:, 2 * i + k, :].bitcast(F32) for k in range(2)])
+            elif op in ("cph", "cpg"):
+                if i not in hg:
+                    hg[i] = work.tile([P, 2, 2 * P, 4], BF16, name="hg", bufs=4, align_bytes=64)
+                drain(eng, trb["tr" + op[2], i], hg[i][:, 0 if op == "cph" else 1])
+            elif op == "qh":
+                s = slice(512 * i, 512 * i + 512)
+                quant(cc[:, s], cs[:, s], hg[i][:].rearrange("p x n j -> p (x n j)"))
+            elif op == "s1":
+                b = psum.tile([P, 4, P], F32, name="s1", bufs=3)
+                s1b[i] = b
+                for t in range(4):
+                    nc.tensor.matmul_mx(
+                        out=b[:, t, :],
+                        lhsT=w2c[:, P * t : P * t + P].bitcast(FP8X4),
+                        lhsT_scale=w2s[:, P * t : P * t + P],
+                        rhs=uc[:, P * i : P * i + P].bitcast(FP8X4),
+                        rhs_scale=us[:, P * i : P * i + P],
+                        start=True,
+                        stop=True,
+                    )
+            elif op == "h2":
+                if i // 2 not in h2g:
+                    h2g[i // 2] = work.tile([P, 2 * P, 4], BF16, name="h2g", bufs=4, align_bytes=64)
+                o = h2g[i // 2][:, P * (i % 2) : P * (i % 2) + P, :]
+                if eng == "v":
+                    nc.vector.tensor_tensor(
+                        out=o, in0=s1b[i][:].rearrange("p t n -> p n t"), in1=b2[:].unsqueeze(1).to_broadcast([P, P, 4]), op=ALU.add
+                    )
+                else:
+                    x = work.tile([P, 4, P], BF16, name="hp", bufs=4, align_bytes=64)
+                    hp[i] = (x, o)
+                    for t in range(4):
+                        nc.scalar.activation(out=x[:, t, :], in_=s1b[i][:, t, :], func=ACT.Identity, bias=b2[:, t : t + 1])
+            elif op == "h2i":
+                x, o = hp[i]
+                nc.vector.tensor_copy(out=o, in_=x[:].rearrange("p t n -> p n t"))
+            elif op == "qh2":
+                s = slice(256 * i, 256 * i + 256)
+                quant(c2[:, s], s2[:, s], h2g[i][:].rearrange("p n j -> p (n j)"))
+            elif op == "s2":
+                b = psum.tile([P, 2, CLS], F32, name="s2", bufs=2)
+                s2b[i] = b
+                for k in range(2):
+                    for c in range(3):
+                        cod, sca, a = (cc, cs, 512 * i + 256 * c + P * k) if c < 2 else (c2, s2, 256 * i + P * k)
+                        nc.tensor.matmul_mx(
+                            out=b[:, k, :],
+                            lhsT=cod[:, a : a + P].bitcast(FP8X4),
+                            lhsT_scale=sca[:, a : a + P],
+                            rhs=woc[:, c, :].bitcast(FP8X4),
+                            rhs_scale=wos[:, c, :],
+                            start=(c == 0),
+                            stop=(c == 2),
+                        )
+            elif op == "lt":
+                nc.vector.tensor_tensor(
+                    out=L[:, 2 * i : 2 * i + 2, :], in0=s2b[i][:], in1=bo[:].unsqueeze(1).to_broadcast([P, 2, CLS]), op=ALU.add
+                )
+            elif op == "mx":
+                nc.vector.tensor_reduce(
+                    out=nmax[:, 2 * i : 2 * i + 2], in_=L[:, 2 * i : 2 * i + 2, :], axis=AX.X, op=ALU.max, negate=True
+                )
+            elif op == "lt1":
+                nc.vector.tensor_tensor(out=L[:, i, :], in0=s2b[i // 2][:, i % 2, :], in1=bo[:], op=ALU.add)
+            elif op == "mx1":
+                nc.vector.tensor_reduce(out=nmax[:, i : i + 1], in_=L[:, i, :], axis=AX.X, op=ALU.max, negate=True)
+            elif op == "ex":
+                e = work.tile([P, CLS], BF16, name="ex", bufs=2)
+                nc.scalar.activation(
+                    out=e[:], in_=L[:, i, :], func=ACT.Exp, bias=nmax[:, i : i + 1], accum_out=sums[:, i : i + 1]
+                )
+            elif op == "ln":
+                a, b = GROUPS[i]
+                nc.scalar.activation(out=lns[:, a:b], in_=sums[:, a:b], func=ACT.Ln)
+            elif op == "sh":
+                a, b = GROUPS[i]
+                nc.vector.tensor_sub(out=shift[:, a:b], in0=nmax[:, a:b], in1=lns[:, a:b])
+            elif op == "fin":
+                if eng == "v":
+                    nc.vector.tensor_scalar(
+                        out=res[:, i, :], in0=L[:, i, :], scalar1=nmax[:, i : i + 1], scalar2=lns[:, i : i + 1], op0=ALU.add, op1=ALU.subtract
+                    )
+                else:
+                    nc.scalar.activation(out=res[:, i, :], in_=L[:, i, :], func=ACT.Identity, bias=shift[:, i : i + 1])
+            elif op == "st":
+                (nc.scalar if eng == "s" else nc.sync).dma_start(out=ov[:, 2 * i : 2 * i + 2, :], in_=res[:, 2 * i : 2 * i + 2, :])
+            else:
+                raise ValueError(op)
+
+        for s in ORDER:
+            a = s.split(".")
+            step(a[0], a[1], int(a[2]))

@@ -17,7 +17,7 @@ N, HID, CLS = 1024, 512, 256
 P = 128
 G = N // P
 ORDER = """ldw2.x.0 ldu.x.0 ldu.x.1 lduh.x.1 ldwo.x.0 ldh.x.0 ldg.x.0 ldwx.x.0 ldh.x.1 ldg.x.1
-scP.p.0 boF.v.0 boP.p.0 sc.s.0 w2i.v.0 w2i.s.1 tt.v.1 w2i.s.3 tt.v.0 bo.s.0 tt.v.5 tru.p.0 w2i.s.2 tt.v.4 woi.s.0 tt.v.3 tru.p.2 tt.v.2 trh.p.0 cpu.s.0 qw2.v.0 cpu.s.2 tru.p.1 qup.v.0 qwo.v.0 cph.s.0 trh.p.1 qup.v.2 tt.v.7 cpu.s.1 s1.p.1 s1.p.4 tt.v.6 woi.s.1 s1.p.5 trg.p.1 h2.v.1 h2.v.5 trh.p.2 woi.s.2 qwo.v.1 s1.p.0 qup.v.1 h2.v.4 s1.p.2 cpg.s.1 qwo.v.2 s1.p.3 cph.s.1 qh2.v.2 trg.p.2 h2.v.0 cph.s.2 tru.p.3 qh.v.1 cpg.s.2 trg.p.3 qh2.v.0 cpu.s.3 h2.v.2 trh.p.3 cpg.s.3 trg.p.0 qh.v.2 cph.s.3 qup.v.3 s2.p.2 h2.v.3 cpg.s.0 qh.v.3 s1.p.6 s1.p.7 lt.v.2 qh.v.0 mx.v.2 s2.p.0 h2.v.6 ex.s.4 ex.s.5 qh2.v.1 h2.v.7 s2.p.1 lt.v.0 qh2.v.3 lt.v.1 s2.p.3 mx.v.0 mx.v.1 ex.s.1 ex.s.0 lt1.v.6 ex.s.2 lt1.v.7 mx1.v.6 ex.s.3 mx1.v.7 ex.s.6 ex.s.7 ln.s.0 fin.v.2 fin.v.3 fin.v.0 fin.v.5 fin.v.4 fin.v.1 sh.v.0 fin.s.6 st.y.1 fin.s.7 st.y.2 st.y.0 st.y.3""".split()
+scP.p.0 boF.v.0 boP.p.0 sc.s.0 w2i.v.0 w2i.s.1 tt.v.0 w2i.s.3 tt.v.1 w2i.s.2 tt.v.2 tru.p.0 tt.v.3 bo.s.0 cpu.s.0 tt.v.5 tru.p.1 tt.v.6 trh.p.1 cpu.s.1 qup.v.0 trh.p.0 tt.v.7 cph.s.1 trg.p.0 qup.v.1 cph.s.0 tt.v.4 tru.p.3 cpg.s.0 trg.p.1 qw2.v.0 cpu.s.3 tru.p.2 woi.v.1 cpg.s.1 s1.p.3 qup.v.3 s1.p.0 cpu.s.2 woi.v.0 s1.p.1 trh.p.2 h2.s.3 qup.v.2 qwo.v.0 trg.p.2 h2.s.0 woi.v.2 s1.p.2 h2.s.1 qh.v.0 s1.p.4 trg.p.3 cph.s.2 h2i.v.0 h2.s.2 s1.p.5 qwo.v.1 trh.p.3 cpg.s.3 qh2.v.0 h2i.v.1 s1.p.6 h2.s.4 qwo.v.2 cph.s.3 s1.p.7 qh2.v.1 s2.p.0 qh.v.1 h2.s.5 qh.v.3 h2.s.6 s2.p.1 h2i.v.2 h2.s.7 lt.v.0 cpg.s.2 h2i.v.3 qh.v.2 qh2.v.2 qh2.v.3 s2.p.2 mx.v.0 lt.v.1 ex.s.0 ex.s.1 lt.v.2 s2.p.3 mx.v.1 mx.v.2 ex.s.2 ex.s.3 lt1.v.6 ex.s.4 lt1.v.7 mx1.v.6 ex.s.5 mx1.v.7 ex.s.6 ex.s.7 ln.s.0 fin.v.0 fin.v.1 fin.v.3 fin.v.4 fin.v.5 sh.v.0 fin.v.2 fin.s.6 st.y.0 fin.s.7 st.y.2 st.y.1 st.y.3""".split()
 GROUPS = [[0,8]]
 FLOPS = 2 * N * HID * HID + 2 * N * 3 * HID * CLS
 
@@ -167,34 +167,35 @@ def tile_gin_pc_kernel(tc, u1_bytes, u1_scale, W2_1, b2_1, h, h1, W_out, b_out, 
                 s = slice(512 * i, 512 * i + 512)
                 quant(cc[:, s], cs[:, s], hg[i][:].rearrange("p x n j -> p (x n j)"))
             elif op == "s1":
-                b = psum.tile([P, 4, P], F32, name="s1", bufs=3)
+                p, tp = divmod(i, 2)
+                b = psum.tile([P, 2, 2 * P], F32, name="s1", bufs=3)
                 s1b[i] = b
-                for t in range(4):
+                for k in range(2):
+                    t = 2 * tp + k
                     nc.tensor.matmul_mx(
-                        out=b[:, t, :],
+                        out=b[:, k, :],
                         lhsT=w2c[:, P * t : P * t + P].bitcast(FP8X4),
                         lhsT_scale=w2s[:, P * t : P * t + P],
-                        rhs=uc[:, P * i : P * i + P].bitcast(FP8X4),
-                        rhs_scale=us[:, P * i : P * i + P],
+                        rhs=uc[:, 256 * p : 256 * p + 256].bitcast(FP8X4),
+                        rhs_scale=us[:, 256 * p : 256 * p + 256],
                         start=True,
                         stop=True,
                     )
             elif op == "h2":
-                if i // 2 not in h2g:
-                    h2g[i // 2] = work.tile([P, 2 * P, 4], BF16, name="h2g", bufs=4, align_bytes=64)
-                o = h2g[i // 2][:, P * (i % 2) : P * (i % 2) + P, :]
-                if eng == "v":
-                    nc.vector.tensor_tensor(
-                        out=o, in0=s1b[i][:].rearrange("p t n -> p n t"), in1=b2[:].unsqueeze(1).to_broadcast([P, P, 4]), op=ALU.add
-                    )
-                else:
-                    x = work.tile([P, 4, P], BF16, name="hp", bufs=4, align_bytes=64)
-                    hp[i] = (x, o)
-                    for t in range(4):
-                        nc.scalar.activation(out=x[:, t, :], in_=s1b[i][:, t, :], func=ACT.Identity, bias=b2[:, t : t + 1])
+                p, tp = divmod(i, 2)
+                if p not in hp:
+                    hp[p] = work.tile([P, 4, 2 * P], BF16, name="hp", bufs=4, align_bytes=64)
+                for k in range(2):
+                    t = 2 * tp + k
+                    if eng == "v":
+                        nc.vector.tensor_scalar(
+                            out=hp[p][:, t, :], in0=s1b[i][:, k, :], scalar1=b2[:, t : t + 1], scalar2=None, op0=ALU.add
+                        )
+                    else:
+                        nc.scalar.activation(out=hp[p][:, t, :], in_=s1b[i][:, k, :], func=ACT.Identity, bias=b2[:, t : t + 1])
             elif op == "h2i":
-                x, o = hp[i]
-                nc.vector.tensor_copy(out=o, in_=x[:].rearrange("p t n -> p n t"))
+                h2g[i] = work.tile([P, 2 * P, 4], BF16, name="h2g", bufs=4, align_bytes=64)
+                cp(eng, h2g[i][:], hp[i][:].rearrange("p t n -> p n t"))
             elif op == "qh2":
                 s = slice(256 * i, 256 * i + 256)
                 quant(c2[:, s], s2[:, s], h2g[i][:].rearrange("p n j -> p (n j)"))

@@ -16,9 +16,11 @@ AX = mybir.AxisListType
 N, HID, CLS = 1024, 512, 256
 P = 128
 G = N // P
-ORDER = """ldw2.x.0 ldu.x.0 ldu.x.1 lduh.x.1 ldwo.x.0 ldh.x.0 ldg.x.0 ldwx.x.0 ldh.x.1 ldg.x.1
-scP.p.0 boF.v.0 boP.p.0 sc.s.0 w2i.v.0 w2i.s.1 tt.v.0 w2i.s.3 tt.v.1 w2i.s.2 tt.v.2 tru.p.0 tt.v.3 bo.s.0 cpu.s.0 tt.v.5 tru.p.1 tt.v.6 trh.p.1 cpu.s.1 qup.v.0 trh.p.0 tt.v.7 cph.s.1 trg.p.0 qup.v.1 cph.s.0 tt.v.4 tru.p.3 cpg.s.0 trg.p.1 qw2.v.0 cpu.s.3 tru.p.2 woi.v.1 cpg.s.1 s1.p.3 qup.v.3 s1.p.0 cpu.s.2 woi.v.0 s1.p.1 trh.p.2 h2.s.3 qup.v.2 qwo.v.0 trg.p.2 h2.s.0 woi.v.2 s1.p.2 h2.s.1 qh.v.0 s1.p.4 trg.p.3 cph.s.2 h2i.v.0 h2.s.2 s1.p.5 qwo.v.1 trh.p.3 cpg.s.3 qh2.v.0 h2i.v.1 s1.p.6 h2.s.4 qwo.v.2 cph.s.3 s1.p.7 qh2.v.1 s2.p.0 qh.v.1 h2.s.5 qh.v.3 h2.s.6 s2.p.1 h2i.v.2 h2.s.7 lt.v.0 cpg.s.2 h2i.v.3 qh.v.2 qh2.v.2 qh2.v.3 s2.p.2 mx.v.0 lt.v.1 ex.s.0 ex.s.1 lt.v.2 s2.p.3 mx.v.1 mx.v.2 ex.s.2 ex.s.3 lt1.v.6 ex.s.4 lt1.v.7 mx1.v.6 ex.s.5 mx1.v.7 ex.s.6 ex.s.7 ln.s.0 fin.v.0 fin.v.1 fin.v.3 fin.v.4 fin.v.5 sh.v.0 fin.v.2 fin.s.6 st.y.0 fin.s.7 st.y.2 st.y.1 st.y.3""".split()
-GROUPS = [[0,8]]
+ORDER = """ldwo.x.0 ldu.x.0 ldw2.x.0 ldu.x.1 lduh.x.1 ldh.x.0 ldg.x.0 ldwx.x.0 ldh.x.1 ldg.x.1
+scP.p.0 boF.v.0 boP.p.0 woi.v.0 sc.s.0 bo.s.0 tt.v.0 tt.v.1 w2i.s.2 tt.v.2 w2i.s.0 tru.p.0 tt.v.3 w2i.s.3 w2i.v.1 tru.p.1 cpu.s.0 tt.v.4 trh.p.0 qw2.v.0 cpu.s.1 trh.p.1 qup.v.0 cph.s.0 trg.p.0 qup.v.1 qwo.v.0 cph.s.1 s1.p.0 tt.v.5 s1.p.1 cpg.s.0 s1.p.2 woi.v.2 tru.p.2 h2.s.0 qh.v.0 h2.s.1 s1.p.3 tt.v.6 trh.p.2 cpu.s.2 tt.v.7 trh.p.3 h2.s.2 woi.v.1 tru.p.3 cph.s.2 h2i.v.0 h2.s.3 trg.p.1 qup.v.2 cpu.s.3 h2i.v.1 s1.p.4 cpg.s.1 s1.p.5 qup.v.3 trg.p.2 h2.s.4 qwo.v.1 qwo.v.2 trg.p.3 h2.s.5 qh.v.1 s1.p.6 cpg.s.2 qh2.v.0 s1.p.7 qh2.v.1 cpg.s.3 s2.p.0 h2i.v.2 h2.s.7 qh.v.2 s2.p.1 h2.s.6 qh2.v.2 lt.v.0 cph.s.3 lt.v.1 s2.p.2 h2i.s.3 qh.v.3 mx.v.0 qh2.v.3 ex.s.1 lt.v.2 s2.p.3 ex.s.0 mx.v.1 lg.d.0 mx.v.2 ex.s.2 ex.s.3 lt1.v.6 ex.s.4 lt1.v.7 lg.d.1 mx1.v.6 ex.s.5 mx1.v.7 ex.s.6 ex.s.7 lx.v.0 lp.v.0 ln.s.1 lp.v.1 lp.v.2 sh.v.0 fin.v.1 fin.v.0 fin.v.3 fin.v.2 sh.v.1 st.y.0 fin.s.7 fin.v.6 fin.s.4 fin.s.5 st.y.1 st.y.3 st.y.2""".split()
+NA = 4
+ROOT = 256
+LN_POLY = (0.9999999969467316, -0.4999986398238411, 0.3331446743250296, -0.23963844080173094)
 FLOPS = 2 * N * HID * HID + 2 * N * 3 * HID * CLS
 
 
@@ -63,9 +65,13 @@ def tile_gin_pc_kernel(tc, u1_bytes, u1_scale, W2_1, b2_1, h, h1, W_out, b_out, 
         sums = kt("sums", [P, G], F32)
         lns = kt("lns", [P, G], F32)
         shift = kt("shift", [P, G], F32)
+        lv, lx = [kt(n, [P, NA], F32) for n in ("lv", "lx")]
+        root = kt("root", [P, 2], F32)
+        nc.gpsimd.memset(root[:], 1 / ROOT)
+        lp = [kt("lp%d" % k, [P, NA], F32) for k in range(3)]
         dummy = kt("dummy", [P, 1], F32)
 
-        nc.scalar.dma_start(out=sccol[:], in_=u1_scale.rearrange("o (p t) -> p (o t)", t=4))
+        nc.sync.dma_start(out=sccol[:], in_=u1_scale.rearrange("o (p t) -> p (o t)", t=4))
         nc.scalar.dma_start(out=bocol[:], in_=b_out.rearrange("(p t) -> p t", t=2))
         nc.scalar.dma_start(out=b2[:], in_=b2_1.rearrange("(p t) -> p t", t=4))
         u1v = u1_bytes.rearrange("(p g) k -> p g k", g=G)
@@ -136,7 +142,7 @@ def tile_gin_pc_kernel(tc, u1_bytes, u1_scale, W2_1, b2_1, h, h1, W_out, b_out, 
             elif op == "w2i":
                 cp(eng, w2g[:, i * P : (i + 1) * P, :], w2r[:].rearrange("p j (m t) -> p t m j", t=4)[:, i])
             elif op == "woi":
-                cp(eng, wog[:, i], wor[:, i].rearrange("p j n -> p n j"))
+                cp(eng, wog[:, i].rearrange("p (c q) j -> p c j q", q=4), wor[:, i].rearrange("p j (c q) -> p c j q", q=4))
             elif op == "qw2":
                 quant(w2c[:], w2s[:], w2g[:].rearrange("p n j -> p (n j)"))
             elif op == "qwo":
@@ -195,7 +201,7 @@ def tile_gin_pc_kernel(tc, u1_bytes, u1_scale, W2_1, b2_1, h, h1, W_out, b_out, 
                         nc.scalar.activation(out=hp[p][:, t, :], in_=s1b[i][:, k, :], func=ACT.Identity, bias=b2[:, t : t + 1])
             elif op == "h2i":
                 h2g[i] = work.tile([P, 2 * P, 4], BF16, name="h2g", bufs=4, align_bytes=64)
-                cp(eng, h2g[i][:], hp[i][:].rearrange("p t n -> p n t"))
+                cp(eng, h2g[i][:].rearrange("p (c q) t -> p c t q", q=4), hp[i][:].rearrange("p t (c q) -> p c t q", q=4))
             elif op == "qh2":
                 s = slice(256 * i, 256 * i + 256)
                 quant(c2[:, s], s2[:, s], h2g[i][:].rearrange("p n j -> p (n j)"))
@@ -232,15 +238,27 @@ def tile_gin_pc_kernel(tc, u1_bytes, u1_scale, W2_1, b2_1, h, h1, W_out, b_out, 
                     out=e[:], in_=L[:, i, :], func=ACT.Exp, bias=nmax[:, i : i + 1], accum_out=sums[:, i : i + 1]
                 )
             elif op == "ln":
-                a, b = GROUPS[i]
-                nc.scalar.activation(out=lns[:, a:b], in_=sums[:, a:b], func=ACT.Ln)
+                nc.scalar.activation(out=lns[:, NA:], in_=sums[:, NA:], func=ACT.Ln)
+            elif op == "lg":
+                p = slice(2 * i, 2 * i + 2)
+                nc.gpsimd.tensor_tensor(out=lv[:, p], in0=sums[:, p], in1=root[:], op=ALU.pow)
+            elif op == "lx":
+                nc.vector.tensor_scalar(out=lx[:], in0=lv[:], scalar1=-1.0, scalar2=None, op0=ALU.add)
+            elif op == "lp":
+                nc.vector.scalar_tensor_tensor(
+                    out=lp[i][:], in0=(lx if i == 0 else lp[i - 1])[:], scalar=LN_POLY[2 - i] / LN_POLY[3], in1=lx[:], op0=ALU.add, op1=ALU.mult
+                )
             elif op == "sh":
-                a, b = GROUPS[i]
-                nc.vector.tensor_sub(out=shift[:, a:b], in0=nmax[:, a:b], in1=lns[:, a:b])
+                if i == 0:
+                    nc.vector.scalar_tensor_tensor(
+                        out=shift[:, :NA], in0=lp[2][:], scalar=-ROOT * LN_POLY[3], in1=nmax[:, :NA], op0=ALU.mult, op1=ALU.add
+                    )
+                else:
+                    nc.vector.tensor_sub(out=shift[:, NA:], in0=nmax[:, NA:], in1=lns[:, NA:])
             elif op == "fin":
                 if eng == "v":
                     nc.vector.tensor_scalar(
-                        out=res[:, i, :], in0=L[:, i, :], scalar1=nmax[:, i : i + 1], scalar2=lns[:, i : i + 1], op0=ALU.add, op1=ALU.subtract
+                        out=res[:, i, :], in0=L[:, i, :], scalar1=shift[:, i : i + 1], scalar2=None, op0=ALU.add
                     )
                 else:
                     nc.scalar.activation(out=res[:, i, :], in_=L[:, i, :], func=ACT.Identity, bias=shift[:, i : i + 1])

@@ -17,7 +17,7 @@ N, HID, CLS = 1024, 512, 256
 P = 128
 G = N // P
 ORDER = """ldwo.x.0 ldu.x.0 ldw2.x.0 ldu.x.1 lduh.x.1 ldh.x.0 ldg.x.0 ldwx.x.0 ldh.x.1 ldg.x.1
-scP.p.0 boF.v.0 boP.p.0 woi.v.0 sc.s.0 bo.s.0 tt.v.0 tt.v.1 w2i.s.2 tt.v.2 w2i.s.0 tru.p.0 tt.v.3 w2i.s.3 w2i.v.1 tru.p.1 cpu.s.0 tt.v.4 trh.p.0 qw2.v.0 cpu.s.1 trh.p.1 qup.v.0 cph.s.0 trg.p.0 qup.v.1 qwo.v.0 cph.s.1 s1.p.0 tt.v.5 s1.p.1 cpg.s.0 s1.p.2 woi.v.2 tru.p.2 h2.s.0 qh.v.0 h2.s.1 s1.p.3 tt.v.6 trh.p.2 cpu.s.2 tt.v.7 trh.p.3 h2.s.2 woi.v.1 tru.p.3 cph.s.2 h2i.v.0 h2.s.3 trg.p.1 qup.v.2 cpu.s.3 h2i.v.1 s1.p.4 cpg.s.1 s1.p.5 qup.v.3 trg.p.2 h2.s.4 qwo.v.1 qwo.v.2 trg.p.3 h2.s.5 qh.v.1 s1.p.6 cpg.s.2 qh2.v.0 s1.p.7 qh2.v.1 cpg.s.3 s2.p.0 h2i.v.2 h2.s.7 qh.v.2 s2.p.1 h2.s.6 qh2.v.2 lt.v.0 cph.s.3 lt.v.1 s2.p.2 h2i.s.3 qh.v.3 mx.v.0 qh2.v.3 ex.s.1 lt.v.2 s2.p.3 ex.s.0 mx.v.1 lg.d.0 mx.v.2 ex.s.2 ex.s.3 lt1.v.6 ex.s.4 lt1.v.7 lg.d.1 mx1.v.6 ex.s.5 mx1.v.7 ex.s.6 ex.s.7 lx.v.0 lp.v.0 ln.s.1 lp.v.1 lp.v.2 sh.v.0 fin.v.1 fin.v.0 fin.v.3 fin.v.2 sh.v.1 st.y.0 fin.s.7 fin.v.6 fin.s.4 fin.s.5 st.y.1 st.y.3 st.y.2""".split()
+scP.p.0 boF.v.0 boP.p.0 woi.v.0 sc.s.0 bo.s.0 qwo.v.0 tt.v.0 w2i.s.1 tt.v.1 w2i.s.3 tt.v.2 tru.p.0 w2i.s.0 tt.v.3 tt.v.4 w2i.s.2 trh.p.0 tt.v.5 cpu.s.0 trh.p.1 tt.v.6 cph.s.0 tru.p.1 tt.v.7 cph.s.1 trg.p.0 qw2.v.0 cpu.s.1 tru.p.2 qup.v.0 cpg.s.0 tru.p.3 woi.v.1 cpu.s.2 s1.p.0 qup.v.1 s1.p.1 cpu.s.3 trh.p.2 qup.v.2 qh.v.0 h2.s.0 trh.p.3 qup.v.3 h2.s.1 s1.p.2 woi.v.2 trg.p.1 cph.s.2 h2i.v.0 h2.s.2 trg.p.2 qwo.v.1 s1.p.3 cpg.s.1 qwo.v.2 qh2.v.0 s1.p.4 cpg.s.2 s1.p.5 qh.v.1 s2.p.0 h2.s.3 qh.v.2 h2.s.4 trg.p.3 h2i.v.1 h2.s.5 s1.p.6 lt.v.0 s1.p.7 cpg.s.3 qh2.v.1 h2i.v.2 h2.s.6 s2.p.1 mx.v.0 h2.s.7 qh2.v.2 cph.s.3 lt.v.1 s2.p.2 h2i.s.3 qh.v.3 mx.v.1 ex.s.0 qh2.v.3 ex.s.1 lt.v.2 s2.p.3 ex.s.3 lg.d.0 ex.s.2 mx.v.2 lg.d.1 lt1.v.6 ex.s.4 lt1.v.7 ex.s.5 mx1.v.6 mx1.v.7 ex.s.6 lx.v.0 ex.s.7 lp.v.0 lp.v.1 ln.s.1 lp.v.2 sh.v.0 fin.v.0 fin.v.2 fin.v.3 fin.v.1 st.y.1 shs.s.4 shs.s.5 shs.s.7 fin.v.4 shs.s.6 fin.v.5 fin.s.7 st.y.0 fin.s.6 st.y.2 st.y.3""".split()
 NA = 4
 ROOT = 256
 LN_POLY = (0.9999999969467316, -0.4999986398238411, 0.3331446743250296, -0.23963844080173094)
@@ -249,12 +249,13 @@ def tile_gin_pc_kernel(tc, u1_bytes, u1_scale, W2_1, b2_1, h, h1, W_out, b_out, 
                     out=lp[i][:], in0=(lx if i == 0 else lp[i - 1])[:], scalar=LN_POLY[2 - i] / LN_POLY[3], in1=lx[:], op0=ALU.add, op1=ALU.mult
                 )
             elif op == "sh":
-                if i == 0:
-                    nc.vector.scalar_tensor_tensor(
-                        out=shift[:, :NA], in0=lp[2][:], scalar=-ROOT * LN_POLY[3], in1=nmax[:, :NA], op0=ALU.mult, op1=ALU.add
-                    )
-                else:
-                    nc.vector.tensor_sub(out=shift[:, NA:], in0=nmax[:, NA:], in1=lns[:, NA:])
+                nc.vector.scalar_tensor_tensor(
+                    out=shift[:, :NA], in0=lp[2][:], scalar=-ROOT * LN_POLY[3], in1=nmax[:, :NA], op0=ALU.mult, op1=ALU.add
+                )
+            elif op == "shs":
+                nc.scalar.activation(
+                    out=shift[:, i : i + 1], in_=lns[:, i : i + 1], func=ACT.Identity, scale=-1.0, bias=nmax[:, i : i + 1]
+                )
             elif op == "fin":
                 if eng == "v":
                     nc.vector.tensor_scalar(

@@ -16,9 +16,10 @@ AX = mybir.AxisListType
 N, HID, CLS = 1024, 512, 256
 P = 128
 G = N // P
-ORDER = """ldwo.x.0 ldu.x.0 ldw2.x.0 ldu.x.1 lduh.x.1 ldh.x.0 ldg.x.0 ldwx.x.0 ldh.x.1 ldg.x.1
-scP.p.0 boF.v.0 boP.p.0 woi.v.0 sc.s.0 bo.s.0 qwo.v.0 tt.v.0 w2i.s.1 tt.v.1 w2i.s.3 tt.v.2 tru.p.0 w2i.s.0 tt.v.3 tt.v.4 w2i.s.2 trh.p.0 tt.v.5 cpu.s.0 trh.p.1 tt.v.6 cph.s.0 tru.p.1 tt.v.7 cph.s.1 trg.p.0 qw2.v.0 cpu.s.1 tru.p.2 qup.v.0 cpg.s.0 tru.p.3 woi.v.1 cpu.s.2 s1.p.0 qup.v.1 s1.p.1 cpu.s.3 trh.p.2 qup.v.2 qh.v.0 h2.s.0 trh.p.3 qup.v.3 h2.s.1 s1.p.2 woi.v.2 trg.p.1 cph.s.2 h2i.v.0 h2.s.2 trg.p.2 qwo.v.1 s1.p.3 cpg.s.1 qwo.v.2 qh2.v.0 s1.p.4 cpg.s.2 s1.p.5 qh.v.1 s2.p.0 h2.s.3 qh.v.2 h2.s.4 trg.p.3 h2i.v.1 h2.s.5 s1.p.6 lt.v.0 s1.p.7 cpg.s.3 qh2.v.1 h2i.v.2 h2.s.6 s2.p.1 mx.v.0 h2.s.7 qh2.v.2 cph.s.3 lt.v.1 s2.p.2 h2i.s.3 qh.v.3 mx.v.1 ex.s.0 qh2.v.3 ex.s.1 lt.v.2 s2.p.3 ex.s.3 lg.d.0 ex.s.2 mx.v.2 lg.d.1 lt1.v.6 ex.s.4 lt1.v.7 ex.s.5 mx1.v.6 mx1.v.7 ex.s.6 lx.v.0 ex.s.7 lp.v.0 lp.v.1 ln.s.1 lp.v.2 sh.v.0 fin.v.0 fin.v.2 fin.v.3 fin.v.1 st.y.1 shs.s.4 shs.s.5 shs.s.7 fin.v.4 shs.s.6 fin.v.5 fin.s.7 st.y.0 fin.s.6 st.y.2 st.y.3""".split()
+ORDER = """ldwo.x.0 ldu.x.0 ldw2.x.0 ldu.x.1 ldh.x.0 lduh.x.1 ldg.x.0 ldwx.x.0 ldh.x.1 ldg.x.1
+wm.p.0 scP.p.0 boF.v.0 boP.p.0 woi.v.0 sc.s.0 qwo.v.0 bo.s.0 tt.v.0 w2i.s.2 tt.v.1 w2i.s.3 tt.v.2 tru.p.0 w2i.s.1 tt.v.3 trh.p.0 w2i.v.0 cpu.s.0 tt.v.4 tru.p.1 qw2.v.0 cph.s.0 trg.p.0 qup.v.0 cpu.s.1 tt.v.5 s1.p.0 tt.v.6 cpg.s.0 s1.p.1 tru.p.2 tt.v.7 h2.s.0 woi.v.1 h2.s.1 tru.p.3 qup.v.1 cpu.s.2 qwo.v.1 trg.p.1 h2i.v.0 cpu.s.3 s1.p.2 qup.v.2 cpg.s.1 s1.p.3 qh.v.0 s1.p.4 h2.s.2 trh.p.1 woi.v.2 h2.s.3 qh2.v.0 trh.p.2 qwo.v.2 h2.s.4 h2i.v.1 s1.p.5 cph.s.1 qup.v.3 s2.p.0 cph.s.2 qh2.v.1 qh.v.1 s1.p.6 h2.s.5 s1.p.7 lt.v.0 s2.p.1 h2.s.6 h2i.v.2 h2.s.7 trg.p.2 mx.v.0 qh2.v.2 trg.p.3 ex.s.1 h2i.v.3 cpg.s.2 trh.p.3 lt.v.1 ex.s.0 cpg.s.3 lg.d.0 qh.v.2 cph.s.3 qh2.v.3 s2.p.2 mx.v.1 qh.v.3 ex.s.2 ex.s.3 lt.v.2 s2.p.3 lg.d.1 mx.v.2 lt1.v.6 ex.s.4 lt1.v.7 ex.s.5 mx1.v.6 mx1.v.7 ex.s.6 lx.v.0 ex.s.7 lp.v.0 lp.v.1 ln.s.1 lp.v.2 sh.v.0 fin.v.0 fin.v.1 st.y.0 fin.v.2 fin.v.3 st.y.1 sh1.v.0 fin.v.6 fin.s.7 st.y.3 fin.v.4 fin.v.5 st.y.2""".split()
 NA = 4
+WARM = 2
 ROOT = 256
 LN_POLY = (0.9999999969467316, -0.4999986398238411, 0.3331446743250296, -0.23963844080173094)
 FLOPS = 2 * N * HID * HID + 2 * N * 3 * HID * CLS
@@ -81,6 +82,8 @@ def tile_gin_pc_kernel(tc, u1_bytes, u1_scale, W2_1, b2_1, h, h1, W_out, b_out, 
         wov = W_out.rearrange("(c p j) n -> p c j n", p=P, j=4)
         w2v = W2_1.rearrange("(p j) n -> p j n", j=4)
 
+        wz = kt("wz", [P, 2 * P], F32)
+        nc.vector.memset(wz[:], 0.0)
         nc.vector.memset(dummy[:], 0.0)
         nc.scalar.activation(out=dummy[:], in_=dummy[:], func=ACT.Exp)
         make_identity(nc, ident[:])
@@ -125,8 +128,13 @@ def tile_gin_pc_kernel(tc, u1_bytes, u1_scale, W2_1, b2_1, h, h1, W_out, b_out, 
                 nc.sync.dma_start(out=wor[:, i], in_=wov[:, i])
             elif op == "ldwx":
                 nc.sync.dma_start(out=wor[:, 1:3], in_=wov[:, 1:3])
-            elif op == "scP":
+            elif op == "wm":
                 trb["sc"] = psum.tile([P, 4, P], F32, name="tr", bufs=3)
+                for k in range(WARM):
+                    nc.tensor.matmul(
+                        trb["sc"][:].rearrange("p t q -> p (t q)"), lhsT=wz[:].bitcast(BF16)[:, 0:P], rhs=wz[:].bitcast(BF16), start=True, stop=True
+                    )
+            elif op == "scP":
                 for t in range(4):
                     nc.tensor.transpose(trb["sc"][:, t, :], sccol[:, t : t + 1].to_broadcast([P, P]), ident[:])
             elif op == "sc":
@@ -252,10 +260,8 @@ def tile_gin_pc_kernel(tc, u1_bytes, u1_scale, W2_1, b2_1, h, h1, W_out, b_out, 
                 nc.vector.scalar_tensor_tensor(
                     out=shift[:, :NA], in0=lp[2][:], scalar=-ROOT * LN_POLY[3], in1=nmax[:, :NA], op0=ALU.mult, op1=ALU.add
                 )
-            elif op == "shs":
-                nc.scalar.activation(
-                    out=shift[:, i : i + 1], in_=lns[:, i : i + 1], func=ACT.Identity, scale=-1.0, bias=nmax[:, i : i + 1]
-                )
+            elif op == "sh1":
+                nc.vector.tensor_sub(out=shift[:, NA:], in0=nmax[:, NA:], in1=lns[:, NA:])
             elif op == "fin":
                 if eng == "v":
                     nc.vector.tensor_scalar(

from contextlib import ExitStack

import concourse.mybir as mybir
from concourse.masks import make_identity

F32 = mybir.dt.float32
BF16 = mybir.dt.bfloat16
U32 = mybir.dt.uint32
U8 = mybir.dt.uint8
FP8 = mybir.dt.float8_e4m3fn
FP8X4 = mybir.dt.float8_e4m3fn_x4
ALU = mybir.AluOpType
ACT = mybir.ActivationFunctionType
AX = mybir.AxisListType

N, HID, CLS = 1024, 512, 256
P = 128
G = N // P
ORDER = """ldwo.x.0 ldu.x.0 ldw2.x.0 ldu.x.1 ldh.x.0 lduh.x.1 ldg.x.0 ldwx.x.0 ldh.x.1 ldg.x.1
wm.p.0 scP.p.0 boF.v.0 boP.p.0 woi.v.0 sc.s.0 qwo.v.0 bo.s.0 tt.v.0 w2i.s.2 tt.v.1 w2i.s.3 tt.v.2 tru.p.0 w2i.s.1 tt.v.3 trh.p.0 w2i.v.0 cpu.s.0 tt.v.4 tru.p.1 qw2.v.0 cph.s.0 trg.p.0 qup.v.0 cpu.s.1 tt.v.5 s1.p.0 tt.v.6 cpg.s.0 s1.p.1 tru.p.2 tt.v.7 h2.s.0 woi.v.1 h2.s.1 tru.p.3 qup.v.1 cpu.s.2 qwo.v.1 trg.p.1 h2i.v.0 cpu.s.3 s1.p.2 qup.v.2 cpg.s.1 s1.p.3 qh.v.0 s1.p.4 h2.s.2 trh.p.1 woi.v.2 h2.s.3 qh2.v.0 trh.p.2 qwo.v.2 h2.s.4 h2i.v.1 s1.p.5 cph.s.1 qup.v.3 s2.p.0 cph.s.2 qh2.v.1 qh.v.1 s1.p.6 h2.s.5 s1.p.7 lt.v.0 s2.p.1 h2.s.6 h2i.v.2 h2.s.7 trg.p.2 mx.v.0 qh2.v.2 trg.p.3 ex.s.1 h2i.v.3 cpg.s.2 trh.p.3 lt.v.1 ex.s.0 cpg.s.3 lg.d.0 qh.v.2 cph.s.3 qh2.v.3 s2.p.2 mx.v.1 qh.v.3 ex.s.2 ex.s.3 lt.v.2 s2.p.3 lg.d.1 mx.v.2 lt1.v.6 ex.s.4 lt1.v.7 ex.s.5 mx1.v.6 mx1.v.7 ex.s.6 lx.v.0 ex.s.7 lp.v.0 lp.v.1 ln.s.1 lp.v.2 sh.v.0 fin.v.0 fin.v.1 st.y.0 fin.v.2 fin.v.3 st.y.1 sh1.v.0 fin.v.6 fin.s.7 st.y.3 fin.v.4 fin.v.5 st.y.2""".split()
NA = 4
WARM = 2
ROOT = 256
LN_POLY = (0.9999999969467316, -0.4999986398238411, 0.3331446743250296, -0.23963844080173094)
FLOPS = 2 * N * HID * HID + 2 * N * 3 * HID * CLS


def tile_gin_pc_kernel(tc, u1_bytes, u1_scale, W2_1, b2_1, h, h1, W_out, b_out, out):
    nc = tc.nc
    with ExitStack() as ctx:
        keep = ctx.enter_context(tc.tile_pool(name="keep", bufs=1))
        work = ctx.enter_context(tc.tile_pool(name="work", bufs=3))
        psum = ctx.enter_context(tc.psum_pool(name="psum", bufs=2))
        ctx.enter_context(tc.manual_schedule())

        def kt(name, shape, dtype):
            return keep.tile(shape, dtype, name=name, align_bytes=64)

        u1b = kt("u1b", [P, G, HID], U8)
        w2r = kt("w2r", [P, 4, HID], BF16)
        wor = kt("wor", [P, 3, 4, CLS], BF16)
        hr = kt("hr", [P, G, HID], BF16)
        h1r = kt("h1r", [P, G, HID], BF16)
        sccol = kt("sccol", [P, 4], F32)
        b2 = kt("b2", [P, 4], BF16)
        bocol = kt("bocol", [P, 2], BF16)
        bocf = kt("bocf", [P, 2], F32)
        sc = kt("sc", [P, HID], F32)
        bo = kt("bo", [P, CLS], F32)
        ident = kt("ident", [P, P], F32)
        w2g = kt("w2g", [P, HID, 4], BF16)
        wog = kt("wog", [P, 3, CLS, 4], BF16)
        w2c = kt("w2c", [P, HID], U32)
        w2s = kt("w2s", [P, HID], U8)
        woc = kt("woc", [P, 3, CLS], U32)
        wos = kt("wos", [P, 3, CLS], U8)
        uc = kt("uc", [P, N], U32)
        us = kt("us", [P, N], U8)
        cc = kt("cc", [P, 2 * N], U32)
        cs = kt("cs", [P, 2 * N], U8)
        c2 = kt("c2", [P, N], U32)
        s2 = kt("s2c", [P, N], U8)
        L = kt("L", [P, G, CLS], F32)
        res = kt("res", [P, G, CLS], F32)
        nmax = kt("nmax", [P, G], F32)
        sums = kt("sums", [P, G], F32)
        lns = kt("lns", [P, G], F32)
        shift = kt("shift", [P, G], F32)
        lv, lx = [kt(n, [P, NA], F32) for n in ("lv", "lx")]
        root = kt("root", [P, 2], F32)
        nc.gpsimd.memset(root[:], 1 / ROOT)
        lp = [kt("lp%d" % k, [P, NA], F32) for k in range(3)]
        dummy = kt("dummy", [P, 1], F32)

        nc.sync.dma_start(out=sccol[:], in_=u1_scale.rearrange("o (p t) -> p (o t)", t=4))
        nc.scalar.dma_start(out=bocol[:], in_=b_out.rearrange("(p t) -> p t", t=2))
        nc.scalar.dma_start(out=b2[:], in_=b2_1.rearrange("(p t) -> p t", t=4))
        u1v = u1_bytes.rearrange("(p g) k -> p g k", g=G)
        hv = h.rearrange("(p g) k -> p g k", g=G)
        h1v = h1.rearrange("(p g) k -> p g k", g=G)
        ov = out.rearrange("(p g) c -> p g c", g=G)
        wov = W_out.rearrange("(c p j) n -> p c j n", p=P, j=4)
        w2v = W2_1.rearrange("(p j) n -> p j n", j=4)

        wz = kt("wz", [P, 2 * P], F32)
        nc.vector.memset(wz[:], 0.0)
        nc.vector.memset(dummy[:], 0.0)
        nc.scalar.activation(out=dummy[:], in_=dummy[:], func=ACT.Exp)
        make_identity(nc, ident[:])

        xs, ug, hg, h2g, s1b, s2b, trb, hp = {}, {}, {}, {}, {}, {}, {}, {}
        raw = [hr, h1r]

        def cp(eng, out, in_):
            if eng == "v":
                nc.vector.tensor_copy(out=out, in_=in_)
            elif eng == "g":
                nc.gpsimd.tensor_scalar(out=out, in0=in_, scalar1=1.0, scalar2=0.0, op0=ALU.mult, op1=ALU.add)
            else:
                nc.scalar.copy(out=out, in_=in_)

        def quant(codes, scales, src):
            nc.vector.quantize_mx(out=codes.bitcast(FP8X4), scales=scales, in_=src)

        def turn(views):
            b = psum.tile([P, len(views), 2, P], F32, name="tr", bufs=3)
            for i, w in enumerate(views):
                for u in range(2):
                    nc.tensor.transpose(b[:, i, u, :], w[:, u : HID // 2 : 2], ident[:])
            return b

        def drain(eng, b, o):
            ow = o.rearrange("p n j -> p (n j)").bitcast(F32).rearrange("p (i r u) -> p i r u", i=2, u=2)
            cp(eng, ow, b[:].rearrange("p i u r -> p i r u"))

        def step(op, eng, i):
            if op == "ldw2":
                nc.sync.dma_start(out=w2r[:], in_=w2v)
            elif op == "ldu":
                nc.sync.dma_start(out=u1b[:, 2 * i : 2 * i + 2, :], in_=u1v[:, 2 * i : 2 * i + 2, :])
            elif op == "lduh":
                nc.sync.dma_start(out=u1b[:, 4 * i : 4 * i + 4, :], in_=u1v[:, 4 * i : 4 * i + 4, :])
            elif op == "ldh":
                nc.sync.dma_start(out=hr[:, 4 * i : 4 * i + 4, :], in_=hv[:, 4 * i : 4 * i + 4, :])
            elif op == "ldg":
                nc.sync.dma_start(out=h1r[:, 4 * i : 4 * i + 4, :], in_=h1v[:, 4 * i : 4 * i + 4, :])
            elif op == "ldwo":
                nc.sync.dma_start(out=wor[:, i], in_=wov[:, i])
            elif op == "ldwx":
                nc.sync.dma_start(out=wor[:, 1:3], in_=wov[:, 1:3])
            elif op == "wm":
                trb["sc"] = psum.tile([P, 4, P], F32, name="tr", bufs=3)
                for k in range(WARM):
                    nc.tensor.matmul(
                        trb["sc"][:].rearrange("p t q -> p (t q)"), lhsT=wz[:].bitcast(BF16)[:, 0:P], rhs=wz[:].bitcast(BF16), start=True, stop=True
                    )
            elif op == "scP":
                for t in range(4):
                    nc.tensor.transpose(trb["sc"][:, t, :], sccol[:, t : t + 1].to_broadcast([P, P]), ident[:])
            elif op == "sc":
                cp(eng, sc[:].rearrange("p (q t) -> p q t", t=4), trb["sc"][:].rearrange("p t q -> p q t"))
            elif op == "boF":
                nc.vector.tensor_copy(out=bocf[:], in_=bocol[:])
            elif op == "boP":
                trb["bo"] = psum.tile([P, 4, P], F32, name="tr", bufs=3)
                for t in range(2):
                    nc.tensor.transpose(trb["bo"][:, t, :], bocf[:, t : t + 1].to_broadcast([P, P]), ident[:])
            elif op == "bo":
                cp(eng, bo[:].rearrange("p (q t) -> p q t", t=2), trb["bo"][:, 0:2, :].rearrange("p t q -> p q t"))
            elif op == "w2i":
                cp(eng, w2g[:, i * P : (i + 1) * P, :], w2r[:].rearrange("p j (m t) -> p t m j", t=4)[:, i])
            elif op == "woi":
                cp(eng, wog[:, i].rearrange("p (c q) j -> p c j q", q=4), wor[:, i].rearrange("p j (c q) -> p c j q", q=4))
            elif op == "qw2":
                quant(w2c[:], w2s[:], w2g[:].rearrange("p n j -> p (n j)"))
            elif op == "qwo":
                quant(woc[:, i, :], wos[:, i, :], wog[:, i].rearrange("p n j -> p (n j)"))
            elif op == "tt":
                xs[i] = work.tile([P, HID], BF16, name="xs", bufs=8, align_bytes=64)
                nc.vector.tensor_tensor(out=xs[i][:], in0=u1b[:, i, :].bitcast(FP8), in1=sc[:], op=ALU.mult)
            elif op == "tru":
                trb["u", i] = turn([xs[2 * i + k][:].bitcast(F32) for k in range(2)])
            elif op == "cpu":
                if i // 2 not in ug:
                    ug[i // 2] = work.tile([P, 4 * P, 4], BF16, name="ug", bufs=2, align_bytes=64)
                drain(eng, trb["u", i], ug[i // 2][:, 2 * P * (i % 2) : 2 * P * (i % 2) + 2 * P, :])
            elif op == "qu":
                s = slice(512 * i, 512 * i + 512)
                quant(uc[:, s], us[:, s], ug[i][:].rearrange("p n j -> p (n j)"))
            elif op == "qup":
                s = slice(256 * i, 256 * i + 256)
                quant(uc[:, s], us[:, s], ug[i // 2][:, 256 * (i % 2) : 256 * (i % 2) + 256, :].rearrange("p n j -> p (n j)"))
            elif op in ("trh", "trg"):
                r = raw[op == "trg"]
                trb[op, i] = turn([r[:, 2 * i + k, :].bitcast(F32) for k in range(2)])
            elif op in ("cph", "cpg"):
                if i not in hg:
                    hg[i] = work.tile([P, 2, 2 * P, 4], BF16, name="hg", bufs=4, align_bytes=64)
                drain(eng, trb["tr" + op[2], i], hg[i][:, 0 if op == "cph" else 1])
            elif op == "qh":
                s = slice(512 * i, 512 * i + 512)
                quant(cc[:, s], cs[:, s], hg[i][:].rearrange("p x n j -> p (x n j)"))
            elif op == "s1":
                p, tp = divmod(i, 2)
                b = psum.tile([P, 2, 2 * P], F32, name="s1", bufs=3)
                s1b[i] = b
                for k in range(2):
                    t = 2 * tp + k
                    nc.tensor.matmul_mx(
                        out=b[:, k, :],
                        lhsT=w2c[:, P * t : P * t + P].bitcast(FP8X4),
                        lhsT_scale=w2s[:, P * t : P * t + P],
                        rhs=uc[:, 256 * p : 256 * p + 256].bitcast(FP8X4),
                        rhs_scale=us[:, 256 * p : 256 * p + 256],
                        start=True,
                        stop=True,
                    )
            elif op == "h2":
                p, tp = divmod(i, 2)
                if p not in hp:
                    hp[p] = work.tile([P, 4, 2 * P], BF16, name="hp", bufs=4, align_bytes=64)
                for k in range(2):
                    t = 2 * tp + k
                    if eng == "v":
                        nc.vector.tensor_scalar(
                            out=hp[p][:, t, :], in0=s1b[i][:, k, :], scalar1=b2[:, t : t + 1], scalar2=None, op0=ALU.add
                        )
                    else:
                        nc.scalar.activation(out=hp[p][:, t, :], in_=s1b[i][:, k, :], func=ACT.Identity, bias=b2[:, t : t + 1])
            elif op == "h2i":
                h2g[i] = work.tile([P, 2 * P, 4], BF16, name="h2g", bufs=4, align_bytes=64)
                cp(eng, h2g[i][:].rearrange("p (c q) t -> p c t q", q=4), hp[i][:].rearrange("p t (c q) -> p c t q", q=4))
            elif op == "qh2":
                s = slice(256 * i, 256 * i + 256)
                quant(c2[:, s], s2[:, s], h2g[i][:].rearrange("p n j -> p (n j)"))
            elif op == "s2":
                b = psum.tile([P, 2, CLS], F32, name="s2", bufs=2)
                s2b[i] = b
                for k in range(2):
                    for c in range(3):
                        cod, sca, a = (cc, cs, 512 * i + 256 * c + P * k) if c < 2 else (c2, s2, 256 * i + P * k)
                        nc.tensor.matmul_mx(
                            out=b[:, k, :],
                            lhsT=cod[:, a : a + P].bitcast(FP8X4),
                            lhsT_scale=sca[:, a : a + P],
                            rhs=woc[:, c, :].bitcast(FP8X4),
                            rhs_scale=wos[:, c, :],
                            start=(c == 0),
                            stop=(c == 2),
                        )
            elif op == "lt":
                nc.vector.tensor_tensor(
                    out=L[:, 2 * i : 2 * i + 2, :], in0=s2b[i][:], in1=bo[:].unsqueeze(1).to_broadcast([P, 2, CLS]), op=ALU.add
                )
            elif op == "mx":
                nc.vector.tensor_reduce(
                    out=nmax[:, 2 * i : 2 * i + 2], in_=L[:, 2 * i : 2 * i + 2, :], axis=AX.X, op=ALU.max, negate=True
                )
            elif op == "lt1":
                nc.vector.tensor_tensor(out=L[:, i, :], in0=s2b[i // 2][:, i % 2, :], in1=bo[:], op=ALU.add)
            elif op == "mx1":
                nc.vector.tensor_reduce(out=nmax[:, i : i + 1], in_=L[:, i, :], axis=AX.X, op=ALU.max, negate=True)
            elif op == "ex":
                e = work.tile([P, CLS], BF16, name="ex", bufs=2)
                nc.scalar.activation(
                    out=e[:], in_=L[:, i, :], func=ACT.Exp, bias=nmax[:, i : i + 1], accum_out=sums[:, i : i + 1]
                )
            elif op == "ln":
                nc.scalar.activation(out=lns[:, NA:], in_=sums[:, NA:], func=ACT.Ln)
            elif op == "lg":
                p = slice(2 * i, 2 * i + 2)
                nc.gpsimd.tensor_tensor(out=lv[:, p], in0=sums[:, p], in1=root[:], op=ALU.pow)
            elif op == "lx":
                nc.vector.tensor_scalar(out=lx[:], in0=lv[:], scalar1=-1.0, scalar2=None, op0=ALU.add)
            elif op == "lp":
                nc.vector.scalar_tensor_tensor(
                    out=lp[i][:], in0=(lx if i == 0 else lp[i - 1])[:], scalar=LN_POLY[2 - i] / LN_POLY[3], in1=lx[:], op0=ALU.add, op1=ALU.mult
                )
            elif op == "sh":
                nc.vector.scalar_tensor_tensor(
                    out=shift[:, :NA], in0=lp[2][:], scalar=-ROOT * LN_POLY[3], in1=nmax[:, :NA], op0=ALU.mult, op1=ALU.add
                )
            elif op == "sh1":
                nc.vector.tensor_sub(out=shift[:, NA:], in0=nmax[:, NA:], in1=lns[:, NA:])
            elif op == "fin":
                if eng == "v":
                    nc.vector.tensor_scalar(
                        out=res[:, i, :], in0=L[:, i, :], scalar1=shift[:, i : i + 1], scalar2=None, op0=ALU.add
                    )
                else:
                    nc.scalar.activation(out=res[:, i, :], in_=L[:, i, :], func=ACT.Identity, bias=shift[:, i : i + 1])
            elif op == "st":
                (nc.scalar if eng == "s" else nc.sync).dma_start(out=ov[:, 2 * i : 2 * i + 2, :], in_=res[:, 2 * i : 2 * i + 2, :])
            else:
                raise ValueError(op)

        for s in ORDER:
            a = s.split(".")
            step(a[0], a[1], int(a[2]))
